import numpy as np
import ml_dtypes


def mxq(x, axis, fmt="e4m3"):
    dtype, down = {"e4m3": (ml_dtypes.float8_e4m3fn, 7), "e5m2": (ml_dtypes.float8_e5m2, 14)}[fmt]
    v = np.moveaxis(np.asarray(x, np.float32).astype(ml_dtypes.bfloat16).astype(np.float64), axis, -1)
    blocks = v.reshape(v.shape[:-1] + (-1, 32))
    amax = np.abs(blocks).max(-1, keepdims=True)
    byte = np.maximum(np.where(amax > 0, np.frexp(amax)[1] - 1 + 127, 0) - down, 1)
    scale = np.exp2(byte - 127.0)
    codes = (blocks / scale).astype(np.float32).astype(dtype).astype(np.float64)
    return np.moveaxis((codes * scale).reshape(v.shape), -1, axis)


WIDE = False


def mx_kscale(k):
    if not WIDE:
        return np.ones(k)
    levels = np.array([10, -10, 5, -5, 0])
    a = np.random.permutation(np.resize(levels, k // 512 * 4)).reshape(k // 512, 4)
    idx = np.arange(k)
    return np.exp2(a[idx // 512, idx % 128 // 32])


BF16 = ml_dtypes.bfloat16


def bf(x):
    return np.asarray(x, np.float32).astype(BF16)


def f64(x):
    return np.asarray(x).astype(np.float64)


B, N, D, GROUP, E1, S1, E2, HID = 4, 32768, 512, 512, 8, 8, 2, 1024
G = N // GROUP
NS = S1 // E2
M = S1 // NS
P2 = E2 * M
R = B * G * M
EPS = 1e-6
LG = 2.0


def l2norm(t):
    return t / np.sqrt(np.sum(t * t, axis=-1, keepdims=True) + EPS)


def setup_inputs():
    s = mx_kscale(D)
    c = np.sqrt(np.mean(1.0 / s**2))
    y = LG / np.sqrt(D) * np.random.standard_normal((B, G, E1, S1, D)) * s * c
    return {"yn": bf(y),
            "means": bf(y.reshape(B, G, E1, M, NS, D).mean(axis=4)),
            "w_slot2": bf(np.random.standard_normal((E1, D, E2 * D)) / s[:, None] / np.tile(s, E2))}


def reference(yn, means, w_slot2):
    mk = f64(means).transpose(2, 0, 1, 3, 4).reshape(E1, R, D)
    se = mxq(mk, 2, "e4m3") @ mxq(f64(w_slot2), 1, "e4m3")
    se = se.reshape(E1, B, G, M, E2, D).transpose(1, 2, 0, 4, 3, 5)
    se2 = (l2norm(se) * np.sqrt(D)).reshape(B, G, E1, P2, D)
    logits = mxq(f64(yn), 4, "e4m3") @ mxq(se2, 4, "e4m3").swapaxes(3, 4)
    a = np.exp(logits - logits.max(axis=3, keepdims=True))
    disp2 = a / a.sum(axis=3, keepdims=True)
    c = np.exp(logits - logits.max(axis=4, keepdims=True))
    comb2 = c / c.sum(axis=4, keepdims=True)
    return disp2, comb2

@@ -1,0 +1,330 @@
+from contextlib import ExitStack
+
+import concourse.mybir as mybir
+from concourse.masks import make_identity
+
+F32 = mybir.dt.float32
+BF16 = mybir.dt.bfloat16
+U32 = mybir.dt.uint32
+U8 = mybir.dt.uint8
+FP8X4 = mybir.dt.float8_e4m3fn_x4
+ALU = mybir.AluOpType
+ACT = mybir.ActivationFunctionType
+AXIS = mybir.AxisListType
+
+P = 128
+PACK = 4
+EXPERTS = 8
+GROUPS = 256
+HALVES = GROUPS // P
+TOKENS = 8
+SEGMENTS = 2
+INNER = 2
+SLOTS = INNER * SEGMENTS
+D = 512
+WORDS = D // 2
+T = 16
+B = GROUPS // T
+LO = B // HALVES
+BANK = 512
+EPS = 1e-6
+
+FLOPS = 2 * EXPERTS * GROUPS * SEGMENTS * D * INNER * D + 2 * EXPERTS * GROUPS * TOKENS * SLOTS * D
+
+
+def tile_hierarchicalsoftmoe2dblock_pb_t_kernel(tc, yn, means, w_slot2, out_0, out_1):
+    nc = tc.nc
+    yn_rows = yn.rearrange("b g k s d -> k (b g) (s d)")
+    means_rows = means.rearrange("b g k m d -> k (b g) (m d)")
+
+    with ExitStack() as ctx:
+        consts = ctx.enter_context(tc.tile_pool(name="consts", bufs=1))
+        first_in = ctx.enter_context(tc.tile_pool(name="first_in", bufs=2))
+        token_in = ctx.enter_context(tc.tile_pool(name="token_in", bufs=2 * HALVES))
+        grouped = ctx.enter_context(tc.tile_pool(name="grouped", bufs=2))
+        packed = ctx.enter_context(tc.tile_pool(name="packed", bufs=2))
+        norms = ctx.enter_context(tc.tile_pool(name="norms", bufs=2))
+        unread = ctx.enter_context(tc.tile_pool(name="unread", bufs=4))
+        picked = ctx.enter_context(tc.tile_pool(name="picked", bufs=2))
+        last = ctx.enter_context(tc.tile_pool(name="last", bufs=1))
+        turned_ps = ctx.enter_context(tc.psum_pool(name="turned_ps", bufs=2))
+        rows_ps = ctx.enter_context(tc.psum_pool(name="rows_ps", bufs=2))
+        cols_ps = ctx.enter_context(tc.psum_pool(name="cols_ps", bufs=2))
+        spread_ps = ctx.enter_context(tc.psum_pool(name="spread_ps", bufs=1))
+        logit_ps = ctx.enter_context(tc.psum_pool(name="logit_ps", bufs=1))
+
+        ident = consts.tile([P, P], F32)
+        make_identity(nc, ident[:])
+        by_t = consts.tile([P, P], F32)
+        nc.vector.tensor_copy(
+            out=by_t[:].rearrange("i (t lo) -> i t lo", t=T),
+            in_=ident[:].rearrange("i (lo t) -> i t lo", t=T),
+        )
+        own_group = consts.tile([P, B], F32)
+        nc.vector.tensor_reduce(
+            out=own_group[:], in_=ident[:].rearrange("q (s b) -> q b s", b=B), axis=AXIS.X, op=ALU.add
+        )
+        logits = consts.tile([P, SLOTS, T * EXPERTS], F32)
+
+        w_raw, m_raw, y_raw = {}, {}, {}
+        w_codes, w_scales, m_codes, m_scales = {}, {}, {}, {}
+        y_codes, y_scales, s_codes, s_scales = {}, {}, {}, {}
+        square_sums, inv_norm, inv_norm_all, se2_grouped = {}, {}, {}, {}
+
+        def load(k):
+            m_in = first_in.tile([P, HALVES, SEGMENTS * D], BF16)
+            nc.sync.dma_start(out=m_in[:], in_=means_rows[k].rearrange("(h p) x -> p h x", p=P))
+            w_in = first_in.tile([P, PACK, INNER * D], BF16)
+            nc.sync.dma_start(
+                out=w_in[:].rearrange("p (u e) c -> p u (e c)", u=2),
+                in_=w_slot2[k].rearrange("(u p e) c -> p u (e c)", u=2, p=P),
+            )
+            m_raw[k], w_raw[k], y_raw[k] = m_in, w_in, []
+            for half in range(HALVES):
+                y_in = token_in.tile([P, TOKENS * D], BF16)
+                nc.sync.dma_start(out=y_in[:], in_=yn_rows[k, half * P : (half + 1) * P, :])
+                y_raw[k].append(y_in)
+
+        def pack_means(k):
+            m_grouped = grouped.tile([P, HALVES * SEGMENTS * P * PACK], BF16, align_bytes=64)
+            m_pairs = m_grouped[:].bitcast(F32).rearrange("p (g c u) -> p g c u", c=P, u=2)
+            m_words = m_raw[k][:].bitcast(F32)
+            for half in range(HALVES):
+                turned = turned_ps.tile([P, SEGMENTS, 2, P], F32)
+                for m in range(SEGMENTS):
+                    for u in range(2):
+                        first = (2 * m + u) * P
+                        nc.tensor.transpose(turned[:, m, u, :], m_words[:, half, first : first + P], by_t[:])
+                nc.scalar.copy(
+                    out=m_pairs[:, SEGMENTS * half : SEGMENTS * (half + 1), :, :],
+                    in_=turned[:].rearrange("p m u c -> p m c u"),
+                )
+            codes = packed.tile([P, HALVES * SEGMENTS * P], U32, align_bytes=64, name="m_codes")
+            scales = packed.tile([P, HALVES * SEGMENTS * P], U8, align_bytes=64, name="m_scales")
+            nc.vector.quantize_mx(out=codes[:].bitcast(FP8X4), scales=scales[:], in_=m_grouped[:])
+            m_codes[k], m_scales[k] = codes, scales
+
+        def pack_w(k):
+            w_grouped = grouped.tile([P, INNER * D * PACK], BF16, align_bytes=64)
+            dst = w_grouped[:].rearrange("p (a odd q j) -> p a q odd j", a=2 * INNER, odd=2, j=PACK)
+            src = w_raw[k][:].rearrange("p j (a q odd) -> p a q odd j", a=2 * INNER, odd=2)
+            codes = packed.tile([P, INNER * D], U32, align_bytes=64, name="w_codes")
+            scales = packed.tile([P, INNER * D], U8, align_bytes=64, name="w_scales")
+            for a in range(2):
+                nc.vector.tensor_copy(out=dst[:, a], in_=src[:, a])
+            for a in range(2, 4):
+                nc.scalar.copy(out=dst[:, a], in_=src[:, a])
+            for e in range(INNER):
+                cols = slice(e * D, (e + 1) * D)
+                nc.vector.quantize_mx(
+                    out=codes[:, cols].bitcast(FP8X4),
+                    scales=scales[:, cols],
+                    in_=w_grouped[:, e * D * PACK : (e + 1) * D * PACK],
+                )
+            w_codes[k], w_scales[k] = codes, scales
+
+        def pack_tokens(k):
+            y_grouped = grouped.tile([P, T * TOKENS * B * PACK], BF16, align_bytes=64)
+            y_pairs = y_grouped[:].bitcast(F32).rearrange("p (t s b u) -> p s t b u", t=T, s=TOKENS, u=2)
+            for half in range(HALVES):
+                y_words = y_raw[k][half][:].bitcast(F32)
+                for s0 in range(0, TOKENS, 2):
+                    turned = turned_ps.tile([P, 2, 2, P], F32)
+                    for s in range(2):
+                        for u in range(2):
+                            first = (2 * (s0 + s) + u) * P
+                            nc.tensor.transpose(turned[:, s, u, :], y_words[:, first : first + P], by_t[:])
+                    nc.scalar.copy(
+                        out=y_pairs[:, s0 : s0 + 2, :, LO * half : LO * (half + 1), :],
+                        in_=turned[:].rearrange("p s u (t lo) -> p s t lo u", t=T),
+                    )
+            codes = packed.tile([P, T * P], U32, align_bytes=64, name="y_codes")
+            scales = packed.tile([P, T * P], U8, align_bytes=64, name="y_scales")
+            for part in range(2):
+                cols = slice(part * T * P // 2, (part + 1) * T * P // 2)
+                nc.vector.quantize_mx(
+                    out=codes[:, cols].bitcast(FP8X4),
+                    scales=scales[:, cols],
+                    in_=y_grouped[:, part * T * P * PACK // 2 : (part + 1) * T * P * PACK // 2],
+                )
+            y_codes[k], y_scales[k] = codes, scales
+
+        def new_square_sums(k):
+            sums = norms.tile([P, HALVES * SEGMENTS * INNER], F32)
+            square_sums[k] = sums
+
+        def new_se2_grouped(k):
+            s_grouped = grouped.tile([P, T * SLOTS * B * PACK], BF16, align_bytes=64)
+            se2_grouped[k] = s_grouped
+
+        def sum_squares(k, g, e):
+            se_rows = rows_ps.tile([P, D], F32)
+            nc.tensor.matmul_mx(
+                out=se_rows[:],
+                lhsT=m_codes[k][:, g * P : (g + 1) * P].bitcast(FP8X4),
+                lhsT_scale=m_scales[k][:, g * P : (g + 1) * P],
+                rhs=w_codes[k][:, e * D : (e + 1) * D].bitcast(FP8X4),
+                rhs_scale=w_scales[k][:, e * D : (e + 1) * D],
+                start=True,
+                stop=True,
+            )
+            squares = unread.tile([P, D], BF16)
+            nc.scalar.activation(
+                out=squares[:],
+                in_=se_rows[:],
+                func=ACT.Square,
+                accum_out=square_sums[k][:, INNER * g + e : INNER * g + e + 1],
+            )
+
+        def invert_norms(k):
+            mean_sq = norms.tile([P, HALVES * SEGMENTS * INNER], F32)
+            nc.vector.tensor_scalar(
+                out=mean_sq[:], in0=square_sums[k][:], scalar1=EPS, scalar2=1.0 / D, op0=ALU.add, op1=ALU.mult
+            )
+            rms = norms.tile([P, HALVES * SEGMENTS * INNER], F32)
+            nc.scalar.sqrt(out=rms[:], in_=mean_sq[:])
+            inv = norms.tile([P, HALVES * SEGMENTS * INNER], F32, name="inv_norm")
+            nc.vector.reciprocal(out=inv[:], in_=rms[:])
+            inv_norm[k] = inv
+
+        def spread_norms(k):
+            everywhere = norms.tile([P, HALVES * SEGMENTS * INNER, P], F32, name="inv_norm_all")
+            per_bank = BANK // P
+            for first in range(0, HALVES * SEGMENTS * INNER, per_bank):
+                spread = spread_ps.tile([P, per_bank, P], F32)
+                for i in range(per_bank):
+                    column = inv_norm[k][:, first + i : first + i + 1]
+                    nc.tensor.transpose(spread[:, i, :], column.to_broadcast([P, P]), ident[:])
+                nc.scalar.copy(out=everywhere[:, first : first + per_bank, :], in_=spread[:])
+            inv_norm_all[k] = everywhere
+
+        def make_slots(k, g, e):
+            half, m = g // SEGMENTS, g % SEGMENTS
+            se_cols = cols_ps.tile([P, PACK, P], F32)
+            for j in range(PACK):
+                chunk = slice((PACK * e + j) * P, (PACK * e + j + 1) * P)
+                nc.tensor.matmul_mx(
+                    out=se_cols[:, j, :],
+                    lhsT=w_codes[k][:, chunk].bitcast(FP8X4),
+                    lhsT_scale=w_scales[k][:, chunk],
+                    rhs=m_codes[k][:, g * P : (g + 1) * P].bitcast(FP8X4),
+                    rhs_scale=m_scales[k][:, g * P : (g + 1) * P],
+                    start=True,
+                    stop=True,
+                )
+            by_column = se2_grouped[k][:].rearrange("p (t slot b j) -> p slot t b j", t=T, slot=SLOTS, j=PACK)
+            scale = inv_norm_all[k][:, INNER * g + e, :].rearrange("p (t lo) -> p t lo", t=T)
+            nc.vector.tensor_tensor(
+                out=by_column[:, SEGMENTS * e + m, :, LO * half : LO * (half + 1), :],
+                in0=se_cols[:].rearrange("p j (t lo) -> p t lo j", t=T),
+                in1=scale.unsqueeze(3).to_broadcast([P, T, LO, PACK]),
+                op=ALU.mult,
+            )
+
+        def pack_slots(k):
+            codes = packed.tile([P, T * SLOTS * B], U32, align_bytes=64, name="s_codes")
+            scales = packed.tile([P, T * SLOTS * B], U8, align_bytes=64, name="s_scales")
+            nc.vector.quantize_mx(out=codes[:].bitcast(FP8X4), scales=scales[:], in_=se2_grouped[k][:])
+            s_codes[k], s_scales[k] = codes, scales
+
+        def multiply_tokens_and_slots(k):
+            per_bank = BANK // (SLOTS * B)
+            for t0 in range(0, T, per_bank):
+                crossed = logit_ps.tile([P, per_bank, SLOTS * B], F32)
+                for i in range(per_bank):
+                    t = t0 + i
+                    nc.tensor.matmul_mx(
+                        out=crossed[:, i, :],
+                        lhsT=y_codes[k][:, t * P : (t + 1) * P].bitcast(FP8X4),
+                        lhsT_scale=y_scales[k][:, t * P : (t + 1) * P],
+                        rhs=s_codes[k][:, t * SLOTS * B : (t + 1) * SLOTS * B].bitcast(FP8X4),
+                        rhs_scale=s_scales[k][:, t * SLOTS * B : (t + 1) * SLOTS * B],
+                        start=True,
+                        stop=True,
+                    )
+                own = picked.tile([P, per_bank * SLOTS, B], F32)
+                nc.vector.tensor_tensor(
+                    out=own[:],
+                    in0=crossed[:].rearrange("q t (slot b) -> q (t slot) b", b=B),
+                    in1=own_group[:].unsqueeze(1).to_broadcast([P, per_bank * SLOTS, B]),
+                    op=ALU.mult,
+                )
+                nc.vector.tensor_reduce(
+                    out=logits[:].rearrange("q slot (t k) -> q slot t k", k=EXPERTS)[:, :, t0 : t0 + per_bank, k],
+                    in_=own[:].rearrange("q (t slot) b -> q slot t b", slot=SLOTS),
+                    axis=AXIS.X,
+                    op=ALU.add,
+                )
+
+        def softmax(label, by_row, reduced, spread_back, out):
+            shape = [P] + [n for n in reduced(by_row).shape[1:-1]]
+            top = last.tile(shape, F32, name="top_" + label)
+            nc.vector.tensor_reduce(out=top[:], in_=reduced(by_row), axis=AXIS.X, op=ALU.max)
+            shifted = last.tile([P, SLOTS, TOKENS, B], F32, name="shifted_" + label)
+            nc.vector.tensor_tensor(out=shifted[:], in0=by_row, in1=spread_back(top[:]), op=ALU.subtract)
+            nc.scalar.activation(out=shifted[:], in_=shifted[:], func=ACT.Exp)
+            total = last.tile(shape, F32, name="total_" + label)
+            nc.vector.tensor_reduce(out=total[:], in_=reduced(shifted[:]), axis=AXIS.X, op=ALU.add)
+            nc.vector.reciprocal(out=total[:], in_=total[:])
+            weights = last.tile([P, B, TOKENS, SLOTS], F32, name="weights_" + label)
+            nc.vector.tensor_tensor(
+                out=weights[:],
+                in0=shifted[:].rearrange("r slot s b -> r b s slot"),
+                in1=spread_back(total[:]).rearrange("r slot s b -> r b s slot"),
+                op=ALU.mult,
+            )
+            nc.sync.dma_start(
+                out=out.rearrange("x g k s slot -> (x g k) (s slot)").rearrange("(b r) w -> r b w", r=P),
+                in_=weights[:].rearrange("r b s slot -> r b (s slot)"),
+            )
+
+        pairs = [(g, e) for g in range(HALVES * SEGMENTS) for e in range(INNER)]
+        load(0)
+        load(1)
+        pack_means(0)
+        pack_w(0)
+        new_square_sums(0)
+        for g, e in pairs:
+            sum_squares(0, g, e)
+        invert_norms(0)
+        for k in range(EXPERTS):
+            following = k + 1 < EXPERTS
+            spread_norms(k)
+            if following:
+                pack_means(k + 1)
+                pack_w(k + 1)
+            pack_tokens(k)
+            if k + 2 < EXPERTS:
+                load(k + 2)
+            if k > 0:
+                multiply_tokens_and_slots(k - 1)
+            new_se2_grouped(k)
+            if following:
+                new_square_sums(k + 1)
+            for g, e in pairs:
+                make_slots(k, g, e)
+                if following:
+                    sum_squares(k + 1, g, e)
+            pack_slots(k)
+            if following:
+                invert_norms(k + 1)
+        multiply_tokens_and_slots(EXPERTS - 1)
+
+        by_row_ps = logit_ps.tile([P, SLOTS, P], F32, tag="crossed")
+        for slot in range(SLOTS):
+            nc.tensor.transpose(by_row_ps[:, slot, :], logits[:, slot, :], ident[:])
+        by_row = by_row_ps[:].rearrange("r slot (s b) -> r slot s b", b=B)
+        softmax(
+            "tokens",
+            by_row,
+            lambda x: x.rearrange("r slot s b -> r slot b s"),
+            lambda x: x.unsqueeze(2).to_broadcast([P, SLOTS, TOKENS, B]),
+            out_0,
+        )
+        softmax(
+            "slots",
+            by_row,
+            lambda x: x.rearrange("r slot s b -> r s b slot"),
+            lambda x: x.unsqueeze(1).to_broadcast([P, SLOTS, TOKENS, B]),
+            out_1,
+        )

@@ -27,6 +27,8 @@ T = 16
 B = GROUPS // T
 LO = B // HALVES
 BANK = 512
+PAIRS = HALVES * SEGMENTS * INNER
+PER_BANK = BANK // P
 EPS = 1e-6
 
 FLOPS = 2 * EXPERTS * GROUPS * SEGMENTS * D * INNER * D + 2 * EXPERTS * GROUPS * TOKENS * SLOTS * D
@@ -42,7 +44,8 @@ def tile_hierarchicalsoftmoe2dblock_pb_t_kernel(tc, yn, means, w_slot2, out_0, o
         first_in = ctx.enter_context(tc.tile_pool(name="first_in", bufs=2))
         token_in = ctx.enter_context(tc.tile_pool(name="token_in", bufs=2 * HALVES))
         grouped = ctx.enter_context(tc.tile_pool(name="grouped", bufs=2))
-        packed = ctx.enter_context(tc.tile_pool(name="packed", bufs=2))
+        packed_first = ctx.enter_context(tc.tile_pool(name="packed_first", bufs=3))
+        packed_second = ctx.enter_context(tc.tile_pool(name="packed_second", bufs=2))
         norms = ctx.enter_context(tc.tile_pool(name="norms", bufs=2))
         unread = ctx.enter_context(tc.tile_pool(name="unread", bufs=4))
         picked = ctx.enter_context(tc.tile_pool(name="picked", bufs=2))
@@ -52,6 +55,7 @@ def tile_hierarchicalsoftmoe2dblock_pb_t_kernel(tc, yn, means, w_slot2, out_0, o
         cols_ps = ctx.enter_context(tc.psum_pool(name="cols_ps", bufs=2))
         spread_ps = ctx.enter_context(tc.psum_pool(name="spread_ps", bufs=1))
         logit_ps = ctx.enter_context(tc.psum_pool(name="logit_ps", bufs=1))
+        ctx.enter_context(tc.manual_schedule())
 
         ident = consts.tile([P, P], F32)
         make_identity(nc, ident[:])
@@ -67,97 +71,139 @@ def tile_hierarchicalsoftmoe2dblock_pb_t_kernel(tc, yn, means, w_slot2, out_0, o
         logits = consts.tile([P, SLOTS, T * EXPERTS], F32)
 
         w_raw, m_raw, y_raw = {}, {}, {}
+        m_grouped, w_grouped, y_grouped, s_grouped = {}, {}, {}, {}
         w_codes, w_scales, m_codes, m_scales = {}, {}, {}, {}
         y_codes, y_scales, s_codes, s_scales = {}, {}, {}, {}
-        square_sums, inv_norm, inv_norm_all, se2_grouped = {}, {}, {}, {}
+        square_sums, link, inv_norm_all = {}, {}, {}
 
-        def load(k):
-            m_in = first_in.tile([P, HALVES, SEGMENTS * D], BF16)
-            nc.sync.dma_start(out=m_in[:], in_=means_rows[k].rearrange("(h p) x -> p h x", p=P))
+        def exists(k):
+            return 0 <= k < EXPERTS
+
+        def load_first(k):
+            if not exists(k):
+                return
             w_in = first_in.tile([P, PACK, INNER * D], BF16)
             nc.sync.dma_start(
                 out=w_in[:].rearrange("p (u e) c -> p u (e c)", u=2),
                 in_=w_slot2[k].rearrange("(u p e) c -> p u (e c)", u=2, p=P),
             )
-            m_raw[k], w_raw[k], y_raw[k] = m_in, w_in, []
+            m_in = first_in.tile([P, HALVES, SEGMENTS * D], BF16)
+            nc.sync.dma_start(out=m_in[:], in_=means_rows[k].rearrange("(h p) x -> p h x", p=P))
+            m_raw[k], w_raw[k] = m_in, w_in
+
+        def load_tokens(k):
+            if not exists(k):
+                return
+            y_raw[k] = []
             for half in range(HALVES):
                 y_in = token_in.tile([P, TOKENS * D], BF16)
                 nc.sync.dma_start(out=y_in[:], in_=yn_rows[k, half * P : (half + 1) * P, :])
                 y_raw[k].append(y_in)
 
-        def pack_means(k):
-            m_grouped = grouped.tile([P, HALVES * SEGMENTS * P * PACK], BF16, align_bytes=64)
-            m_pairs = m_grouped[:].bitcast(F32).rearrange("p (g c u) -> p g c u", c=P, u=2)
+        def copy_turned(filling, out, in_):
+            if filling:
+                nc.vector.tensor_copy(out=out, in_=in_)
+            else:
+                nc.scalar.copy(out=out, in_=in_)
+
+        def turn_means(k, half, filling):
+            if not exists(k):
+                return
+            if half == 0:
+                m_new = grouped.tile([P, HALVES * SEGMENTS * P * PACK], BF16, align_bytes=64, name="m_grouped")
+                m_grouped[k] = m_new
+            m_pairs = m_grouped[k][:].bitcast(F32).rearrange("p (g c u) -> p g c u", c=P, u=2)
             m_words = m_raw[k][:].bitcast(F32)
-            for half in range(HALVES):
-                turned = turned_ps.tile([P, SEGMENTS, 2, P], F32)
-                for m in range(SEGMENTS):
-                    for u in range(2):
-                        first = (2 * m + u) * P
-                        nc.tensor.transpose(turned[:, m, u, :], m_words[:, half, first : first + P], by_t[:])
-                nc.scalar.copy(
-                    out=m_pairs[:, SEGMENTS * half : SEGMENTS * (half + 1), :, :],
-                    in_=turned[:].rearrange("p m u c -> p m c u"),
-                )
-            codes = packed.tile([P, HALVES * SEGMENTS * P], U32, align_bytes=64, name="m_codes")
-            scales = packed.tile([P, HALVES * SEGMENTS * P], U8, align_bytes=64, name="m_scales")
-            nc.vector.quantize_mx(out=codes[:].bitcast(FP8X4), scales=scales[:], in_=m_grouped[:])
+            turned = turned_ps.tile([P, SEGMENTS, 2, P], F32)
+            for m in range(SEGMENTS):
+                for u in range(2):
+                    first = (2 * m + u) * P
+                    nc.tensor.transpose(turned[:, m, u, :], m_words[:, half, first : first + P], by_t[:])
+            copy_turned(
+                filling,
+                out=m_pairs[:, SEGMENTS * half : SEGMENTS * (half + 1), :, :],
+                in_=turned[:].rearrange("p m u c -> p m c u"),
+            )
+
+        def quantise_means(k):
+            if not exists(k):
+                return
+            codes = packed_first.tile([P, HALVES * SEGMENTS * P], U32, align_bytes=64, name="m_codes")
+            scales = packed_first.tile([P, HALVES * SEGMENTS * P], U8, align_bytes=64, name="m_scales")
+            nc.vector.quantize_mx(out=codes[:].bitcast(FP8X4), scales=scales[:], in_=m_grouped[k][:])
             m_codes[k], m_scales[k] = codes, scales
 
-        def pack_w(k):
-            w_grouped = grouped.tile([P, INNER * D * PACK], BF16, align_bytes=64)
-            dst = w_grouped[:].rearrange("p (a odd q j) -> p a q odd j", a=2 * INNER, odd=2, j=PACK)
+        def regroup_w(k):
+            if not exists(k):
+                return
+            w_new = grouped.tile([P, INNER * D * PACK], BF16, align_bytes=64, name="w_grouped")
+            dst = w_new[:].rearrange("p (a odd q j) -> p a q odd j", a=2 * INNER, odd=2, j=PACK)
             src = w_raw[k][:].rearrange("p j (a q odd) -> p a q odd j", a=2 * INNER, odd=2)
-            codes = packed.tile([P, INNER * D], U32, align_bytes=64, name="w_codes")
-            scales = packed.tile([P, INNER * D], U8, align_bytes=64, name="w_scales")
-            for a in range(2):
-                nc.vector.tensor_copy(out=dst[:, a], in_=src[:, a])
-            for a in range(2, 4):
-                nc.scalar.copy(out=dst[:, a], in_=src[:, a])
-            for e in range(INNER):
-                cols = slice(e * D, (e + 1) * D)
-                nc.vector.quantize_mx(
-                    out=codes[:, cols].bitcast(FP8X4),
-                    scales=scales[:, cols],
-                    in_=w_grouped[:, e * D * PACK : (e + 1) * D * PACK],
-                )
-            w_codes[k], w_scales[k] = codes, scales
-
-        def pack_tokens(k):
-            y_grouped = grouped.tile([P, T * TOKENS * B * PACK], BF16, align_bytes=64)
-            y_pairs = y_grouped[:].bitcast(F32).rearrange("p (t s b u) -> p s t b u", t=T, s=TOKENS, u=2)
-            for half in range(HALVES):
-                y_words = y_raw[k][half][:].bitcast(F32)
-                for s0 in range(0, TOKENS, 2):
-                    turned = turned_ps.tile([P, 2, 2, P], F32)
-                    for s in range(2):
-                        for u in range(2):
-                            first = (2 * (s0 + s) + u) * P
-                            nc.tensor.transpose(turned[:, s, u, :], y_words[:, first : first + P], by_t[:])
-                    nc.scalar.copy(
-                        out=y_pairs[:, s0 : s0 + 2, :, LO * half : LO * (half + 1), :],
-                        in_=turned[:].rearrange("p s u (t lo) -> p s t lo u", t=T),
+            for a in range(2 * INNER):
+                if k > 0:
+                    nc.gpsimd.tensor_scalar(
+                        out=dst[:, a], in0=src[:, a], scalar1=1.0, scalar2=0.0, op0=ALU.mult, op1=ALU.add
                     )
-            codes = packed.tile([P, T * P], U32, align_bytes=64, name="y_codes")
-            scales = packed.tile([P, T * P], U8, align_bytes=64, name="y_scales")
-            for part in range(2):
-                cols = slice(part * T * P // 2, (part + 1) * T * P // 2)
-                nc.vector.quantize_mx(
-                    out=codes[:, cols].bitcast(FP8X4),
-                    scales=scales[:, cols],
-                    in_=y_grouped[:, part * T * P * PACK // 2 : (part + 1) * T * P * PACK // 2],
-                )
-            y_codes[k], y_scales[k] = codes, scales
+                elif a % 2 == 0:
+                    nc.vector.tensor_copy(out=dst[:, a], in_=src[:, a])
+                else:
+                    nc.scalar.copy(out=dst[:, a], in_=src[:, a])
+            w_grouped[k] = w_new
 
-        def new_square_sums(k):
-            sums = norms.tile([P, HALVES * SEGMENTS * INNER], F32)
-            square_sums[k] = sums
+        def quantise_w(k, e):
+            if not exists(k):
+                return
+            if e == 0:
+                codes = packed_first.tile([P, INNER * D], U32, align_bytes=64, name="w_codes")
+                scales = packed_first.tile([P, INNER * D], U8, align_bytes=64, name="w_scales")
+                w_codes[k], w_scales[k] = codes, scales
+            nc.vector.quantize_mx(
+                out=w_codes[k][:, e * D : (e + 1) * D].bitcast(FP8X4),
+                scales=w_scales[k][:, e * D : (e + 1) * D],
+                in_=w_grouped[k][:, e * D * PACK : (e + 1) * D * PACK],
+            )
 
-        def new_se2_grouped(k):
-            s_grouped = grouped.tile([P, T * SLOTS * B * PACK], BF16, align_bytes=64)
-            se2_grouped[k] = s_grouped
+        def turn_tokens(k, i, filling):
+            if not exists(k):
+                return
+            half, s0 = i // (TOKENS // 2), 2 * (i % (TOKENS // 2))
+            if i == 0:
+                y_new = grouped.tile([P, T * TOKENS * B * PACK], BF16, align_bytes=64, name="y_grouped")
+                y_grouped[k] = y_new
+            y_pairs = y_grouped[k][:].bitcast(F32).rearrange("p (t s b u) -> p s t b u", t=T, s=TOKENS, u=2)
+            y_words = y_raw[k][half][:].bitcast(F32)
+            turned = turned_ps.tile([P, 2, 2, P], F32)
+            for s in range(2):
+                for u in range(2):
+                    first = (2 * (s0 + s) + u) * P
+                    nc.tensor.transpose(turned[:, s, u, :], y_words[:, first : first + P], by_t[:])
+            copy_turned(
+                filling,
+                out=y_pairs[:, s0 : s0 + 2, :, LO * half : LO * (half + 1), :],
+                in_=turned[:].rearrange("p s u (t lo) -> p s t lo u", t=T),
+            )
 
-        def sum_squares(k, g, e):
+        def quantise_tokens(k, part):
+            if not exists(k):
+                return
+            if part == 0:
+                codes = packed_second.tile([P, T * P], U32, align_bytes=64, name="y_codes")
+                scales = packed_second.tile([P, T * P], U8, align_bytes=64, name="y_scales")
+                y_codes[k], y_scales[k] = codes, scales
+            width = T * P // 2
+            nc.vector.quantize_mx(
+                out=y_codes[k][:, part * width : (part + 1) * width].bitcast(FP8X4),
+                scales=y_scales[k][:, part * width : (part + 1) * width],
+                in_=y_grouped[k][:, part * width * PACK : (part + 1) * width * PACK],
+            )
+
+        def sum_squares(k, i):
+            if not exists(k):
+                return
+            e, g = i // PER_BANK, i % PER_BANK
+            if i == 0:
+                sums = norms.tile([P, PAIRS], F32)
+                square_sums[k] = sums
             se_rows = rows_ps.tile([P, D], F32)
             nc.tensor.matmul_mx(
                 out=se_rows[:],
@@ -170,36 +216,56 @@ def tile_hierarchicalsoftmoe2dblock_pb_t_kernel(tc, yn, means, w_slot2, out_0, o
             )
             squares = unread.tile([P, D], BF16)
             nc.scalar.activation(
-                out=squares[:],
-                in_=se_rows[:],
-                func=ACT.Square,
-                accum_out=square_sums[k][:, INNER * g + e : INNER * g + e + 1],
+                out=squares[:], in_=se_rows[:], func=ACT.Square, accum_out=square_sums[k][:, i : i + 1]
             )
 
-        def invert_norms(k):
-            mean_sq = norms.tile([P, HALVES * SEGMENTS * INNER], F32)
+        def mean_squares(k, part):
+            if not exists(k):
+                return
+            mean_sq = norms.tile([P, PER_BANK], F32)
             nc.vector.tensor_scalar(
-                out=mean_sq[:], in0=square_sums[k][:], scalar1=EPS, scalar2=1.0 / D, op0=ALU.add, op1=ALU.mult
+                out=mean_sq[:],
+                in0=square_sums[k][:, part * PER_BANK : (part + 1) * PER_BANK],
+                scalar1=EPS,
+                scalar2=1.0 / D,
+                op0=ALU.add,
+                op1=ALU.mult,
             )
-            rms = norms.tile([P, HALVES * SEGMENTS * INNER], F32)
-            nc.scalar.sqrt(out=rms[:], in_=mean_sq[:])
-            inv = norms.tile([P, HALVES * SEGMENTS * INNER], F32, name="inv_norm")
-            nc.vector.reciprocal(out=inv[:], in_=rms[:])
-            inv_norm[k] = inv
+            link[k, part] = mean_sq
 
-        def spread_norms(k):
-            everywhere = norms.tile([P, HALVES * SEGMENTS * INNER, P], F32, name="inv_norm_all")
-            per_bank = BANK // P
-            for first in range(0, HALVES * SEGMENTS * INNER, per_bank):
-                spread = spread_ps.tile([P, per_bank, P], F32)
-                for i in range(per_bank):
-                    column = inv_norm[k][:, first + i : first + i + 1]
-                    nc.tensor.transpose(spread[:, i, :], column.to_broadcast([P, P]), ident[:])
-                nc.scalar.copy(out=everywhere[:, first : first + per_bank, :], in_=spread[:])
-            inv_norm_all[k] = everywhere
+        def roots(k, part):
+            if not exists(k):
+                return
+            rms = norms.tile([P, PER_BANK], F32)
+            nc.scalar.sqrt(out=rms[:], in_=link[k, part][:])
+            link[k, part] = rms
 
-        def make_slots(k, g, e):
+        def inverses(k, part):
+            if not exists(k):
+                return
+            inv_norm = norms.tile([P, PER_BANK], F32)
+            nc.vector.reciprocal(out=inv_norm[:], in_=link[k, part][:])
+            link[k, part] = inv_norm
+
+        def spread_norms(k, part):
+            if not exists(k):
+                return
+            if part == 0:
+                everywhere = norms.tile([P, PAIRS, P], F32)
+                inv_norm_all[k] = everywhere
+            spread = spread_ps.tile([P, PER_BANK, P], F32)
+            for i in range(PER_BANK):
+                nc.tensor.transpose(spread[:, i, :], link[k, part][:, i : i + 1].to_broadcast([P, P]), ident[:])
+            nc.scalar.copy(out=inv_norm_all[k][:, part * PER_BANK : (part + 1) * PER_BANK, :], in_=spread[:])
+
+        def make_slots(k, i):
+            if not exists(k):
+                return
+            e, g = i // PER_BANK, i % PER_BANK
             half, m = g // SEGMENTS, g % SEGMENTS
+            if i == 0:
+                s_new = grouped.tile([P, T * SLOTS * B * PACK], BF16, align_bytes=64, name="s_grouped")
+                s_grouped[k] = s_new
             se_cols = cols_ps.tile([P, PACK, P], F32)
             for j in range(PACK):
                 chunk = slice((PACK * e + j) * P, (PACK * e + j + 1) * P)
@@ -212,8 +278,8 @@ def tile_hierarchicalsoftmoe2dblock_pb_t_kernel(tc, yn, means, w_slot2, out_0, o
                     start=True,
                     stop=True,
                 )
-            by_column = se2_grouped[k][:].rearrange("p (t slot b j) -> p slot t b j", t=T, slot=SLOTS, j=PACK)
-            scale = inv_norm_all[k][:, INNER * g + e, :].rearrange("p (t lo) -> p t lo", t=T)
+            by_column = s_grouped[k][:].rearrange("p (t slot b j) -> p slot t b j", t=T, slot=SLOTS, j=PACK)
+            scale = inv_norm_all[k][:, i, :].rearrange("p (t lo) -> p t lo", t=T)
             nc.vector.tensor_tensor(
                 out=by_column[:, SEGMENTS * e + m, :, LO * half : LO * (half + 1), :],
                 in0=se_cols[:].rearrange("p j (t lo) -> p t lo j", t=T),
@@ -221,40 +287,55 @@ def tile_hierarchicalsoftmoe2dblock_pb_t_kernel(tc, yn, means, w_slot2, out_0, o
                 op=ALU.mult,
             )
 
-        def pack_slots(k):
-            codes = packed.tile([P, T * SLOTS * B], U32, align_bytes=64, name="s_codes")
-            scales = packed.tile([P, T * SLOTS * B], U8, align_bytes=64, name="s_scales")
-            nc.vector.quantize_mx(out=codes[:].bitcast(FP8X4), scales=scales[:], in_=se2_grouped[k][:])
-            s_codes[k], s_scales[k] = codes, scales
+        def quantise_slots(k, part):
+            if not exists(k):
+                return
+            if part == 0:
+                codes = packed_second.tile([P, T * SLOTS * B], U32, align_bytes=64, name="s_codes")
+                scales = packed_second.tile([P, T * SLOTS * B], U8, align_bytes=64, name="s_scales")
+                s_codes[k], s_scales[k] = codes, scales
+            width = T * SLOTS * B // 2
+            nc.vector.quantize_mx(
+                out=s_codes[k][:, part * width : (part + 1) * width].bitcast(FP8X4),
+                scales=s_scales[k][:, part * width : (part + 1) * width],
+                in_=s_grouped[k][:, part * width * PACK : (part + 1) * width * PACK],
+            )
 
-        def multiply_tokens_and_slots(k):
-            per_bank = BANK // (SLOTS * B)
-            for t0 in range(0, T, per_bank):
-                crossed = logit_ps.tile([P, per_bank, SLOTS * B], F32)
-                for i in range(per_bank):
-                    t = t0 + i
-                    nc.tensor.matmul_mx(
-                        out=crossed[:, i, :],
-                        lhsT=y_codes[k][:, t * P : (t + 1) * P].bitcast(FP8X4),
-                        lhsT_scale=y_scales[k][:, t * P : (t + 1) * P],
-                        rhs=s_codes[k][:, t * SLOTS * B : (t + 1) * SLOTS * B].bitcast(FP8X4),
-                        rhs_scale=s_scales[k][:, t * SLOTS * B : (t + 1) * SLOTS * B],
-                        start=True,
-                        stop=True,
-                    )
-                own = picked.tile([P, per_bank * SLOTS, B], F32)
-                nc.vector.tensor_tensor(
-                    out=own[:],
-                    in0=crossed[:].rearrange("q t (slot b) -> q (t slot) b", b=B),
-                    in1=own_group[:].unsqueeze(1).to_broadcast([P, per_bank * SLOTS, B]),
-                    op=ALU.mult,
+        def cross(k, part):
+            if not exists(k):
+                return
+            t0 = part * T // 2
+            crossed = logit_ps.tile([P, T // 2, SLOTS * B], F32)
+            for i in range(T // 2):
+                t = t0 + i
+                nc.tensor.matmul_mx(
+                    out=crossed[:, i, :],
+                    lhsT=y_codes[k][:, t * P : (t + 1) * P].bitcast(FP8X4),
+                    lhsT_scale=y_scales[k][:, t * P : (t + 1) * P],
+                    rhs=s_codes[k][:, t * SLOTS * B : (t + 1) * SLOTS * B].bitcast(FP8X4),
+                    rhs_scale=s_scales[k][:, t * SLOTS * B : (t + 1) * SLOTS * B],
+                    start=True,
+                    stop=True,
                 )
-                nc.vector.tensor_reduce(
-                    out=logits[:].rearrange("q slot (t k) -> q slot t k", k=EXPERTS)[:, :, t0 : t0 + per_bank, k],
-                    in_=own[:].rearrange("q (t slot) b -> q slot t b", slot=SLOTS),
-                    axis=AXIS.X,
-                    op=ALU.add,
-                )
+            return crossed
+
+        def pick(k, part, crossed):
+            if not exists(k):
+                return
+            t0 = part * T // 2
+            own = picked.tile([P, T // 2 * SLOTS, B], F32)
+            nc.vector.tensor_tensor(
+                out=own[:],
+                in0=crossed[:].rearrange("q t (slot b) -> q (t slot) b", b=B),
+                in1=own_group[:].unsqueeze(1).to_broadcast([P, T // 2 * SLOTS, B]),
+                op=ALU.mult,
+            )
+            nc.vector.tensor_reduce(
+                out=logits[:].rearrange("q slot (t k) -> q slot t k", k=EXPERTS)[:, :, t0 : t0 + T // 2, k],
+                in_=own[:].rearrange("q (t slot) b -> q slot t b", slot=SLOTS),
+                axis=AXIS.X,
+                op=ALU.add,
+            )
 
         def softmax(label, by_row, reduced, spread_back, out):
             shape = [P] + [n for n in reduced(by_row).shape[1:-1]]
@@ -278,37 +359,68 @@ def tile_hierarchicalsoftmoe2dblock_pb_t_kernel(tc, yn, means, w_slot2, out_0, o
                 in_=weights[:].rearrange("r b s slot -> r b (s slot)"),
             )
 
-        pairs = [(g, e) for g in range(HALVES * SEGMENTS) for e in range(INNER)]
-        load(0)
-        load(1)
-        pack_means(0)
-        pack_w(0)
-        new_square_sums(0)
-        for g, e in pairs:
-            sum_squares(0, g, e)
-        invert_norms(0)
-        for k in range(EXPERTS):
-            following = k + 1 < EXPERTS
-            spread_norms(k)
-            if following:
-                pack_means(k + 1)
-                pack_w(k + 1)
-            pack_tokens(k)
-            if k + 2 < EXPERTS:
-                load(k + 2)
-            if k > 0:
-                multiply_tokens_and_slots(k - 1)
-            new_se2_grouped(k)
-            if following:
-                new_square_sums(k + 1)
-            for g, e in pairs:
-                make_slots(k, g, e)
-                if following:
-                    sum_squares(k + 1, g, e)
-            pack_slots(k)
-            if following:
-                invert_norms(k + 1)
-        multiply_tokens_and_slots(EXPERTS - 1)
+        load_first(0)
+        load_tokens(0)
+        load_first(1)
+        for k in range(-2, EXPERTS + 1):
+            filling = k < 0
+            regroup_w(k + 2)
+
+            make_slots(k, 0)
+            sum_squares(k + 1, 0)
+            turn_tokens(k + 1, 0, filling)
+            mean_squares(k, 1)
+            quantise_slots(k - 1, 0)
+
+            make_slots(k, 1)
+            sum_squares(k + 1, 1)
+            crossed = cross(k - 1, 0)
+            turn_tokens(k + 1, 1, filling)
+            roots(k, 1)
+            quantise_slots(k - 1, 1)
+
+            make_slots(k, 2)
+            sum_squares(k + 1, 2)
+            turn_tokens(k + 1, 2, filling)
+            inverses(k, 1)
+            quantise_tokens(k, 0)
+
+            make_slots(k, 3)
+            sum_squares(k + 1, 3)
+            turn_tokens(k + 1, 3, filling)
+            spread_norms(k, 1)
+            pick(k - 1, 0, crossed)
+
+            make_slots(k, 4)
+            sum_squares(k + 1, 4)
+            crossed = cross(k - 1, 1)
+            turn_tokens(k + 1, 4, filling)
+            turn_means(k + 2, 0, filling)
+            mean_squares(k + 1, 0)
+            quantise_tokens(k, 1)
+
+            make_slots(k, 5)
+            sum_squares(k + 1, 5)
+            turn_tokens(k + 1, 5, filling)
+            turn_means(k + 2, 1, filling)
+            roots(k + 1, 0)
+            quantise_w(k + 2, 0)
+
+            make_slots(k, 6)
+            sum_squares(k + 1, 6)
+            turn_tokens(k + 1, 6, filling)
+            inverses(k + 1, 0)
+            pick(k - 1, 1, crossed)
+
+            make_slots(k, 7)
+            sum_squares(k + 1, 7)
+            turn_tokens(k + 1, 7, filling)
+            spread_norms(k + 1, 0)
+            quantise_means(k + 2)
+            quantise_w(k + 2, 1)
+
+            load_tokens(k + 3)
+            load_first(k + 4)
 
         by_row_ps = logit_ps.tile([P, SLOTS, P], F32, tag="crossed")
         for slot in range(SLOTS):

@@ -133,22 +133,18 @@ def tile_hierarchicalsoftmoe2dblock_pb_t_kernel(tc, yn, means, w_slot2, out_0, o
             nc.vector.quantize_mx(out=codes[:].bitcast(FP8X4), scales=scales[:], in_=m_grouped[k][:])
             m_codes[k], m_scales[k] = codes, scales
 
-        def regroup_w(k):
+        def regroup_w(k, a):
             if not exists(k):
                 return
-            w_new = grouped.tile([P, INNER * D * PACK], BF16, align_bytes=64, name="w_grouped")
-            dst = w_new[:].rearrange("p (a odd q j) -> p a q odd j", a=2 * INNER, odd=2, j=PACK)
+            if a == 0:
+                w_new = grouped.tile([P, INNER * D * PACK], BF16, align_bytes=64, name="w_grouped")
+                w_grouped[k] = w_new
+            dst = w_grouped[k][:].rearrange("p (a odd q j) -> p a q odd j", a=2 * INNER, odd=2, j=PACK)
             src = w_raw[k][:].rearrange("p j (a q odd) -> p a q odd j", a=2 * INNER, odd=2)
-            for a in range(2 * INNER):
-                if k > 0:
-                    nc.gpsimd.tensor_scalar(
-                        out=dst[:, a], in0=src[:, a], scalar1=1.0, scalar2=0.0, op0=ALU.mult, op1=ALU.add
-                    )
-                elif a % 2 == 0:
-                    nc.vector.tensor_copy(out=dst[:, a], in_=src[:, a])
-                else:
-                    nc.scalar.copy(out=dst[:, a], in_=src[:, a])
-            w_grouped[k] = w_new
+            if a % 2 == 0:
+                nc.vector.tensor_copy(out=dst[:, a], in_=src[:, a])
+            else:
+                nc.scalar.copy(out=dst[:, a], in_=src[:, a])
 
         def quantise_w(k, e):
             if not exists(k):
@@ -337,40 +333,18 @@ def tile_hierarchicalsoftmoe2dblock_pb_t_kernel(tc, yn, means, w_slot2, out_0, o
                 op=ALU.add,
             )
 
-        def softmax(label, by_row, reduced, spread_back, out):
-            shape = [P] + [n for n in reduced(by_row).shape[1:-1]]
-            top = last.tile(shape, F32, name="top_" + label)
-            nc.vector.tensor_reduce(out=top[:], in_=reduced(by_row), axis=AXIS.X, op=ALU.max)
-            shifted = last.tile([P, SLOTS, TOKENS, B], F32, name="shifted_" + label)
-            nc.vector.tensor_tensor(out=shifted[:], in0=by_row, in1=spread_back(top[:]), op=ALU.subtract)
-            nc.scalar.activation(out=shifted[:], in_=shifted[:], func=ACT.Exp)
-            total = last.tile(shape, F32, name="total_" + label)
-            nc.vector.tensor_reduce(out=total[:], in_=reduced(shifted[:]), axis=AXIS.X, op=ALU.add)
-            nc.vector.reciprocal(out=total[:], in_=total[:])
-            weights = last.tile([P, B, TOKENS, SLOTS], F32, name="weights_" + label)
-            nc.vector.tensor_tensor(
-                out=weights[:],
-                in0=shifted[:].rearrange("r slot s b -> r b s slot"),
-                in1=spread_back(total[:]).rearrange("r slot s b -> r b s slot"),
-                op=ALU.mult,
-            )
-            nc.sync.dma_start(
-                out=out.rearrange("x g k s slot -> (x g k) (s slot)").rearrange("(b r) w -> r b w", r=P),
-                in_=weights[:].rearrange("r b s slot -> r b (s slot)"),
-            )
-
         load_first(0)
         load_tokens(0)
         load_first(1)
         for k in range(-2, EXPERTS + 1):
             filling = k < 0
-            regroup_w(k + 2)
 
             make_slots(k, 0)
             sum_squares(k + 1, 0)
             turn_tokens(k + 1, 0, filling)
             mean_squares(k, 1)
             quantise_slots(k - 1, 0)
+            regroup_w(k + 2, 0)
 
             make_slots(k, 1)
             sum_squares(k + 1, 1)
@@ -378,18 +352,21 @@ def tile_hierarchicalsoftmoe2dblock_pb_t_kernel(tc, yn, means, w_slot2, out_0, o
             turn_tokens(k + 1, 1, filling)
             roots(k, 1)
             quantise_slots(k - 1, 1)
+            regroup_w(k + 2, 1)
 
             make_slots(k, 2)
             sum_squares(k + 1, 2)
             turn_tokens(k + 1, 2, filling)
             inverses(k, 1)
             quantise_tokens(k, 0)
+            regroup_w(k + 2, 2)
 
             make_slots(k, 3)
             sum_squares(k + 1, 3)
             turn_tokens(k + 1, 3, filling)
             spread_norms(k, 1)
             pick(k - 1, 0, crossed)
+            regroup_w(k + 2, 3)
 
             make_slots(k, 4)
             sum_squares(k + 1, 4)
@@ -426,17 +403,44 @@ def tile_hierarchicalsoftmoe2dblock_pb_t_kernel(tc, yn, means, w_slot2, out_0, o
         for slot in range(SLOTS):
             nc.tensor.transpose(by_row_ps[:, slot, :], logits[:, slot, :], ident[:])
         by_row = by_row_ps[:].rearrange("r slot (s b) -> r slot s b", b=B)
-        softmax(
-            "tokens",
-            by_row,
-            lambda x: x.rearrange("r slot s b -> r slot b s"),
-            lambda x: x.unsqueeze(2).to_broadcast([P, SLOTS, TOKENS, B]),
+        full = [P, SLOTS, TOKENS, B]
+        over_tokens = (
             out_0,
+            lambda x: x.rearrange("r slot s b -> r slot b s"),
+            [P, SLOTS, B],
+            lambda x: x.unsqueeze(2).to_broadcast(full),
         )
-        softmax(
-            "slots",
-            by_row,
-            lambda x: x.rearrange("r slot s b -> r s b slot"),
-            lambda x: x.unsqueeze(1).to_broadcast([P, SLOTS, TOKENS, B]),
+        over_slots = (
             out_1,
+            lambda x: x.rearrange("r slot s b -> r s b slot"),
+            [P, TOKENS, B],
+            lambda x: x.unsqueeze(1).to_broadcast(full),
         )
+        both = (over_tokens, over_slots)
+        tops, shifteds, totals = [], [], []
+        for out, index_last, reduced_shape, repeated in both:
+            top = last.tile(reduced_shape, F32, bufs=2)
+            nc.vector.tensor_reduce(out=top[:], in_=index_last(by_row), axis=AXIS.X, op=ALU.max)
+            tops.append(top)
+        for (out, index_last, reduced_shape, repeated), top in zip(both, tops):
+            shifted = last.tile(full, F32, bufs=2)
+            nc.vector.tensor_tensor(out=shifted[:], in0=by_row, in1=repeated(top[:]), op=ALU.subtract)
+            nc.scalar.activation(out=shifted[:], in_=shifted[:], func=ACT.Exp)
+            shifteds.append(shifted)
+        for (out, index_last, reduced_shape, repeated), shifted in zip(both, shifteds):
+            total = last.tile(reduced_shape, F32, bufs=2)
+            nc.vector.tensor_reduce(out=total[:], in_=index_last(shifted[:]), axis=AXIS.X, op=ALU.add)
+            nc.vector.reciprocal(out=total[:], in_=total[:])
+            totals.append(total)
+        for (out, index_last, reduced_shape, repeated), shifted, total in zip(both, shifteds, totals):
+            weights = last.tile([P, B, TOKENS, SLOTS], F32, bufs=2)
+            nc.vector.tensor_tensor(
+                out=weights[:],
+                in0=shifted[:].rearrange("r slot s b -> r b s slot"),
+                in1=repeated(total[:]).rearrange("r slot s b -> r b s slot"),
+                op=ALU.mult,
+            )
+            nc.sync.dma_start(
+                out=out.rearrange("x g k s slot -> (x g k) (s slot)").rearrange("(b r) w -> r b w", r=P),
+                in_=weights[:].rearrange("r b s slot -> r b (s slot)"),
+            )

from contextlib import ExitStack

import concourse.mybir as mybir
from concourse.masks import make_identity

F32 = mybir.dt.float32
BF16 = mybir.dt.bfloat16
U32 = mybir.dt.uint32
U8 = mybir.dt.uint8
FP8X4 = mybir.dt.float8_e4m3fn_x4
ALU = mybir.AluOpType
ACT = mybir.ActivationFunctionType
AXIS = mybir.AxisListType

P = 128
PACK = 4
EXPERTS = 8
GROUPS = 256
HALVES = GROUPS // P
TOKENS = 8
SEGMENTS = 2
INNER = 2
SLOTS = INNER * SEGMENTS
D = 512
WORDS = D // 2
T = 16
B = GROUPS // T
LO = B // HALVES
BANK = 512
PAIRS = HALVES * SEGMENTS * INNER
PER_BANK = BANK // P
EPS = 1e-6

FLOPS = 2 * EXPERTS * GROUPS * SEGMENTS * D * INNER * D + 2 * EXPERTS * GROUPS * TOKENS * SLOTS * D


def tile_hierarchicalsoftmoe2dblock_pb_t_kernel(tc, yn, means, w_slot2, out_0, out_1):
    nc = tc.nc
    yn_rows = yn.rearrange("b g k s d -> k (b g) (s d)")
    means_rows = means.rearrange("b g k m d -> k (b g) (m d)")

    with ExitStack() as ctx:
        consts = ctx.enter_context(tc.tile_pool(name="consts", bufs=1))
        first_in = ctx.enter_context(tc.tile_pool(name="first_in", bufs=2))
        token_in = ctx.enter_context(tc.tile_pool(name="token_in", bufs=2 * HALVES))
        grouped = ctx.enter_context(tc.tile_pool(name="grouped", bufs=2))
        packed_first = ctx.enter_context(tc.tile_pool(name="packed_first", bufs=3))
        packed_second = ctx.enter_context(tc.tile_pool(name="packed_second", bufs=2))
        norms = ctx.enter_context(tc.tile_pool(name="norms", bufs=2))
        unread = ctx.enter_context(tc.tile_pool(name="unread", bufs=4))
        picked = ctx.enter_context(tc.tile_pool(name="picked", bufs=2))
        last = ctx.enter_context(tc.tile_pool(name="last", bufs=1))
        turned_ps = ctx.enter_context(tc.psum_pool(name="turned_ps", bufs=2))
        rows_ps = ctx.enter_context(tc.psum_pool(name="rows_ps", bufs=2))
        cols_ps = ctx.enter_context(tc.psum_pool(name="cols_ps", bufs=2))
        spread_ps = ctx.enter_context(tc.psum_pool(name="spread_ps", bufs=1))
        logit_ps = ctx.enter_context(tc.psum_pool(name="logit_ps", bufs=1))
        ctx.enter_context(tc.manual_schedule())

        ident = consts.tile([P, P], F32)
        make_identity(nc, ident[:])
        by_t = consts.tile([P, P], F32)
        nc.vector.tensor_copy(
            out=by_t[:].rearrange("i (t lo) -> i t lo", t=T),
            in_=ident[:].rearrange("i (lo t) -> i t lo", t=T),
        )
        own_group = consts.tile([P, B], F32)
        nc.vector.tensor_reduce(
            out=own_group[:], in_=ident[:].rearrange("q (s b) -> q b s", b=B), axis=AXIS.X, op=ALU.add
        )
        logits = consts.tile([P, SLOTS, T * EXPERTS], F32)

        w_raw, m_raw, y_raw = {}, {}, {}
        m_grouped, w_grouped, y_grouped, s_grouped = {}, {}, {}, {}
        w_codes, w_scales, m_codes, m_scales = {}, {}, {}, {}
        y_codes, y_scales, s_codes, s_scales = {}, {}, {}, {}
        square_sums, link, inv_norm_all = {}, {}, {}

        def exists(k):
            return 0 <= k < EXPERTS

        def load_first(k):
            if not exists(k):
                return
            w_in = first_in.tile([P, PACK, INNER * D], BF16)
            nc.sync.dma_start(
                out=w_in[:].rearrange("p (u e) c -> p u (e c)", u=2),
                in_=w_slot2[k].rearrange("(u p e) c -> p u (e c)", u=2, p=P),
            )
            m_in = first_in.tile([P, HALVES, SEGMENTS * D], BF16)
            nc.sync.dma_start(out=m_in[:], in_=means_rows[k].rearrange("(h p) x -> p h x", p=P))
            m_raw[k], w_raw[k] = m_in, w_in

        def load_tokens(k):
            if not exists(k):
                return
            y_raw[k] = []
            for half in range(HALVES):
                y_in = token_in.tile([P, TOKENS * D], BF16)
                nc.sync.dma_start(out=y_in[:], in_=yn_rows[k, half * P : (half + 1) * P, :])
                y_raw[k].append(y_in)

        def copy_turned(filling, out, in_):
            if filling:
                nc.vector.tensor_copy(out=out, in_=in_)
            else:
                nc.scalar.copy(out=out, in_=in_)

        def turn_means(k, half, filling):
            if not exists(k):
                return
            if half == 0:
                m_new = grouped.tile([P, HALVES * SEGMENTS * P * PACK], BF16, align_bytes=64, name="m_grouped")
                m_grouped[k] = m_new
            m_pairs = m_grouped[k][:].bitcast(F32).rearrange("p (g c u) -> p g c u", c=P, u=2)
            m_words = m_raw[k][:].bitcast(F32)
            turned = turned_ps.tile([P, SEGMENTS, 2, P], F32)
            for m in range(SEGMENTS):
                for u in range(2):
                    first = (2 * m + u) * P
                    nc.tensor.transpose(turned[:, m, u, :], m_words[:, half, first : first + P], by_t[:])
            copy_turned(
                filling,
                out=m_pairs[:, SEGMENTS * half : SEGMENTS * (half + 1), :, :],
                in_=turned[:].rearrange("p m u c -> p m c u"),
            )

        def quantise_means(k):
            if not exists(k):
                return
            codes = packed_first.tile([P, HALVES * SEGMENTS * P], U32, align_bytes=64, name="m_codes")
            scales = packed_first.tile([P, HALVES * SEGMENTS * P], U8, align_bytes=64, name="m_scales")
            nc.vector.quantize_mx(out=codes[:].bitcast(FP8X4), scales=scales[:], in_=m_grouped[k][:])
            m_codes[k], m_scales[k] = codes, scales

        def regroup_w(k, a):
            if not exists(k):
                return
            if a == 0:
                w_new = grouped.tile([P, INNER * D * PACK], BF16, align_bytes=64, name="w_grouped")
                w_grouped[k] = w_new
            dst = w_grouped[k][:].rearrange("p (a odd q j) -> p a q odd j", a=2 * INNER, odd=2, j=PACK)
            src = w_raw[k][:].rearrange("p j (a q odd) -> p a q odd j", a=2 * INNER, odd=2)
            if a % 2 == 0:
                nc.vector.tensor_copy(out=dst[:, a], in_=src[:, a])
            else:
                nc.scalar.copy(out=dst[:, a], in_=src[:, a])

        def quantise_w(k, e):
            if not exists(k):
                return
            if e == 0:
                codes = packed_first.tile([P, INNER * D], U32, align_bytes=64, name="w_codes")
                scales = packed_first.tile([P, INNER * D], U8, align_bytes=64, name="w_scales")
                w_codes[k], w_scales[k] = codes, scales
            nc.vector.quantize_mx(
                out=w_codes[k][:, e * D : (e + 1) * D].bitcast(FP8X4),
                scales=w_scales[k][:, e * D : (e + 1) * D],
                in_=w_grouped[k][:, e * D * PACK : (e + 1) * D * PACK],
            )

        def turn_tokens(k, i, filling):
            if not exists(k):
                return
            half, s0 = i // (TOKENS // 2), 2 * (i % (TOKENS // 2))
            if i == 0:
                y_new = grouped.tile([P, T * TOKENS * B * PACK], BF16, align_bytes=64, name="y_grouped")
                y_grouped[k] = y_new
            y_pairs = y_grouped[k][:].bitcast(F32).rearrange("p (t s b u) -> p s t b u", t=T, s=TOKENS, u=2)
            y_words = y_raw[k][half][:].bitcast(F32)
            turned = turned_ps.tile([P, 2, 2, P], F32)
            for s in range(2):
                for u in range(2):
                    first = (2 * (s0 + s) + u) * P
                    nc.tensor.transpose(turned[:, s, u, :], y_words[:, first : first + P], by_t[:])
            copy_turned(
                filling,
                out=y_pairs[:, s0 : s0 + 2, :, LO * half : LO * (half + 1), :],
                in_=turned[:].rearrange("p s u (t lo) -> p s t lo u", t=T),
            )

        def quantise_tokens(k, part):
            if not exists(k):
                return
            if part == 0:
                codes = packed_second.tile([P, T * P], U32, align_bytes=64, name="y_codes")
                scales = packed_second.tile([P, T * P], U8, align_bytes=64, name="y_scales")
                y_codes[k], y_scales[k] = codes, scales
            width = T * P // 2
            nc.vector.quantize_mx(
                out=y_codes[k][:, part * width : (part + 1) * width].bitcast(FP8X4),
                scales=y_scales[k][:, part * width : (part + 1) * width],
                in_=y_grouped[k][:, part * width * PACK : (part + 1) * width * PACK],
            )

        def sum_squares(k, i):
            if not exists(k):
                return
            e, g = i // PER_BANK, i % PER_BANK
            if i == 0:
                sums = norms.tile([P, PAIRS], F32)
                square_sums[k] = sums
            se_rows = rows_ps.tile([P, D], F32)
            nc.tensor.matmul_mx(
                out=se_rows[:],
                lhsT=m_codes[k][:, g * P : (g + 1) * P].bitcast(FP8X4),
                lhsT_scale=m_scales[k][:, g * P : (g + 1) * P],
                rhs=w_codes[k][:, e * D : (e + 1) * D].bitcast(FP8X4),
                rhs_scale=w_scales[k][:, e * D : (e + 1) * D],
                start=True,
                stop=True,
            )
            squares = unread.tile([P, D], BF16)
            nc.scalar.activation(
                out=squares[:], in_=se_rows[:], func=ACT.Square, accum_out=square_sums[k][:, i : i + 1]
            )

        def mean_squares(k, part):
            if not exists(k):
                return
            mean_sq = norms.tile([P, PER_BANK], F32)
            nc.vector.tensor_scalar(
                out=mean_sq[:],
                in0=square_sums[k][:, part * PER_BANK : (part + 1) * PER_BANK],
                scalar1=EPS,
                scalar2=1.0 / D,
                op0=ALU.add,
                op1=ALU.mult,
            )
            link[k, part] = mean_sq

        def roots(k, part):
            if not exists(k):
                return
            rms = norms.tile([P, PER_BANK], F32)
            nc.scalar.sqrt(out=rms[:], in_=link[k, part][:])
            link[k, part] = rms

        def inverses(k, part):
            if not exists(k):
                return
            inv_norm = norms.tile([P, PER_BANK], F32)
            nc.vector.reciprocal(out=inv_norm[:], in_=link[k, part][:])
            link[k, part] = inv_norm

        def spread_norms(k, part):
            if not exists(k):
                return
            if part == 0:
                everywhere = norms.tile([P, PAIRS, P], F32)
                inv_norm_all[k] = everywhere
            spread = spread_ps.tile([P, PER_BANK, P], F32)
            for i in range(PER_BANK):
                nc.tensor.transpose(spread[:, i, :], link[k, part][:, i : i + 1].to_broadcast([P, P]), ident[:])
            nc.scalar.copy(out=inv_norm_all[k][:, part * PER_BANK : (part + 1) * PER_BANK, :], in_=spread[:])

        def make_slots(k, i):
            if not exists(k):
                return
            e, g = i // PER_BANK, i % PER_BANK
            half, m = g // SEGMENTS, g % SEGMENTS
            if i == 0:
                s_new = grouped.tile([P, T * SLOTS * B * PACK], BF16, align_bytes=64, name="s_grouped")
                s_grouped[k] = s_new
            se_cols = cols_ps.tile([P, PACK, P], F32)
            for j in range(PACK):
                chunk = slice((PACK * e + j) * P, (PACK * e + j + 1) * P)
                nc.tensor.matmul_mx(
                    out=se_cols[:, j, :],
                    lhsT=w_codes[k][:, chunk].bitcast(FP8X4),
                    lhsT_scale=w_scales[k][:, chunk],
                    rhs=m_codes[k][:, g * P : (g + 1) * P].bitcast(FP8X4),
                    rhs_scale=m_scales[k][:, g * P : (g + 1) * P],
                    start=True,
                    stop=True,
                )
            by_column = s_grouped[k][:].rearrange("p (t slot b j) -> p slot t b j", t=T, slot=SLOTS, j=PACK)
            scale = inv_norm_all[k][:, i, :].rearrange("p (t lo) -> p t lo", t=T)
            nc.vector.tensor_tensor(
                out=by_column[:, SEGMENTS * e + m, :, LO * half : LO * (half + 1), :],
                in0=se_cols[:].rearrange("p j (t lo) -> p t lo j", t=T),
                in1=scale.unsqueeze(3).to_broadcast([P, T, LO, PACK]),
                op=ALU.mult,
            )

        def quantise_slots(k, part):
            if not exists(k):
                return
            if part == 0:
                codes = packed_second.tile([P, T * SLOTS * B], U32, align_bytes=64, name="s_codes")
                scales = packed_second.tile([P, T * SLOTS * B], U8, align_bytes=64, name="s_scales")
                s_codes[k], s_scales[k] = codes, scales
            width = T * SLOTS * B // 2
            nc.vector.quantize_mx(
                out=s_codes[k][:, part * width : (part + 1) * width].bitcast(FP8X4),
                scales=s_scales[k][:, part * width : (part + 1) * width],
                in_=s_grouped[k][:, part * width * PACK : (part + 1) * width * PACK],
            )

        def cross(k, part):
            if not exists(k):
                return
            t0 = part * T // 2
            crossed = logit_ps.tile([P, T // 2, SLOTS * B], F32)
            for i in range(T // 2):
                t = t0 + i
                nc.tensor.matmul_mx(
                    out=crossed[:, i, :],
                    lhsT=y_codes[k][:, t * P : (t + 1) * P].bitcast(FP8X4),
                    lhsT_scale=y_scales[k][:, t * P : (t + 1) * P],
                    rhs=s_codes[k][:, t * SLOTS * B : (t + 1) * SLOTS * B].bitcast(FP8X4),
                    rhs_scale=s_scales[k][:, t * SLOTS * B : (t + 1) * SLOTS * B],
                    start=True,
                    stop=True,
                )
            return crossed

        def pick(k, part, crossed):
            if not exists(k):
                return
            t0 = part * T // 2
            own = picked.tile([P, T // 2 * SLOTS, B], F32)
            nc.vector.tensor_tensor(
                out=own[:],
                in0=crossed[:].rearrange("q t (slot b) -> q (t slot) b", b=B),
                in1=own_group[:].unsqueeze(1).to_broadcast([P, T // 2 * SLOTS, B]),
                op=ALU.mult,
            )
            nc.vector.tensor_reduce(
                out=logits[:].rearrange("q slot (t k) -> q slot t k", k=EXPERTS)[:, :, t0 : t0 + T // 2, k],
                in_=own[:].rearrange("q (t slot) b -> q slot t b", slot=SLOTS),
                axis=AXIS.X,
                op=ALU.add,
            )

        load_first(0)
        load_tokens(0)
        load_first(1)
        for k in range(-2, EXPERTS + 1):
            filling = k < 0

            make_slots(k, 0)
            sum_squares(k + 1, 0)
            turn_tokens(k + 1, 0, filling)
            mean_squares(k, 1)
            quantise_slots(k - 1, 0)
            regroup_w(k + 2, 0)

            make_slots(k, 1)
            sum_squares(k + 1, 1)
            crossed = cross(k - 1, 0)
            turn_tokens(k + 1, 1, filling)
            roots(k, 1)
            quantise_slots(k - 1, 1)
            regroup_w(k + 2, 1)

            make_slots(k, 2)
            sum_squares(k + 1, 2)
            turn_tokens(k + 1, 2, filling)
            inverses(k, 1)
            quantise_tokens(k, 0)
            regroup_w(k + 2, 2)

            make_slots(k, 3)
            sum_squares(k + 1, 3)
            turn_tokens(k + 1, 3, filling)
            spread_norms(k, 1)
            pick(k - 1, 0, crossed)
            regroup_w(k + 2, 3)

            make_slots(k, 4)
            sum_squares(k + 1, 4)
            crossed = cross(k - 1, 1)
            turn_tokens(k + 1, 4, filling)
            turn_means(k + 2, 0, filling)
            mean_squares(k + 1, 0)
            quantise_tokens(k, 1)

            make_slots(k, 5)
            sum_squares(k + 1, 5)
            turn_tokens(k + 1, 5, filling)
            turn_means(k + 2, 1, filling)
            roots(k + 1, 0)
            quantise_w(k + 2, 0)

            make_slots(k, 6)
            sum_squares(k + 1, 6)
            turn_tokens(k + 1, 6, filling)
            inverses(k + 1, 0)
            pick(k - 1, 1, crossed)

            make_slots(k, 7)
            sum_squares(k + 1, 7)
            turn_tokens(k + 1, 7, filling)
            spread_norms(k + 1, 0)
            quantise_means(k + 2)
            quantise_w(k + 2, 1)

            load_tokens(k + 3)
            load_first(k + 4)

        by_row_ps = logit_ps.tile([P, SLOTS, P], F32, tag="crossed")
        for slot in range(SLOTS):
            nc.tensor.transpose(by_row_ps[:, slot, :], logits[:, slot, :], ident[:])
        by_row = by_row_ps[:].rearrange("r slot (s b) -> r slot s b", b=B)
        full = [P, SLOTS, TOKENS, B]
        over_tokens = (
            out_0,
            lambda x: x.rearrange("r slot s b -> r slot b s"),
            [P, SLOTS, B],
            lambda x: x.unsqueeze(2).to_broadcast(full),
        )
        over_slots = (
            out_1,
            lambda x: x.rearrange("r slot s b -> r s b slot"),
            [P, TOKENS, B],
            lambda x: x.unsqueeze(1).to_broadcast(full),
        )
        both = (over_tokens, over_slots)
        tops, shifteds, totals = [], [], []
        for out, index_last, reduced_shape, repeated in both:
            top = last.tile(reduced_shape, F32, bufs=2)
            nc.vector.tensor_reduce(out=top[:], in_=index_last(by_row), axis=AXIS.X, op=ALU.max)
            tops.append(top)
        for (out, index_last, reduced_shape, repeated), top in zip(both, tops):
            shifted = last.tile(full, F32, bufs=2)
            nc.vector.tensor_tensor(out=shifted[:], in0=by_row, in1=repeated(top[:]), op=ALU.subtract)
            nc.scalar.activation(out=shifted[:], in_=shifted[:], func=ACT.Exp)
            shifteds.append(shifted)
        for (out, index_last, reduced_shape, repeated), shifted in zip(both, shifteds):
            total = last.tile(reduced_shape, F32, bufs=2)
            nc.vector.tensor_reduce(out=total[:], in_=index_last(shifted[:]), axis=AXIS.X, op=ALU.add)
            nc.vector.reciprocal(out=total[:], in_=total[:])
            totals.append(total)
        for (out, index_last, reduced_shape, repeated), shifted, total in zip(both, shifteds, totals):
            weights = last.tile([P, B, TOKENS, SLOTS], F32, bufs=2)
            nc.vector.tensor_tensor(
                out=weights[:],
                in0=shifted[:].rearrange("r slot s b -> r b s slot"),
                in1=repeated(total[:]).rearrange("r slot s b -> r b s slot"),
                op=ALU.mult,
            )
            nc.sync.dma_start(
                out=out.rearrange("x g k s slot -> (x g k) (s slot)").rearrange("(b r) w -> r b w", r=P),
                in_=weights[:].rearrange("r b s slot -> r b (s slot)"),
            )
